import numpy as np
import ml_dtypes


def mxq(x, axis, fmt="e4m3"):
    dtype, down = {"e4m3": (ml_dtypes.float8_e4m3fn, 7), "e5m2": (ml_dtypes.float8_e5m2, 14)}[fmt]
    v = np.moveaxis(np.asarray(x, np.float32).astype(ml_dtypes.bfloat16).astype(np.float64), axis, -1)
    blocks = v.reshape(v.shape[:-1] + (-1, 32))
    amax = np.abs(blocks).max(-1, keepdims=True)
    byte = np.maximum(np.where(amax > 0, np.frexp(amax)[1] - 1 + 127, 0) - down, 1)
    scale = np.exp2(byte - 127.0)
    codes = (blocks / scale).astype(np.float32).astype(dtype).astype(np.float64)
    return np.moveaxis((codes * scale).reshape(v.shape), -1, axis)


WIDE = False


def mx_kscale(k):
    if not WIDE:
        return np.ones(k)
    levels = np.array([10, -10, 5, -5, 0])
    a = np.random.permutation(np.resize(levels, k // 512 * 4)).reshape(k // 512, 4)
    idx = np.arange(k)
    return np.exp2(a[idx // 512, idx % 128 // 32])


BF16 = ml_dtypes.bfloat16


def bf(x):
    return np.asarray(x, np.float32).astype(BF16)


def f64(x):
    return np.asarray(x).astype(np.float64)


B, N, R, I = 2, 2048, 128, 256
SIG = 1.5
P0 = 0.05
RM = np.exp(0.5 * SIG * SIG)


def draw_flows():
    keep = np.random.random((B, 1, N)) >= P0
    return keep * np.exp(SIG * np.random.standard_normal((B, N, N)) - 0.5 * SIG * SIG)


def setup_inputs():
    u = mx_kscale(N)
    return {"flows": bf(draw_flows() * u[None, :, None]),
            "x_gcn1": bf(np.random.standard_normal((B, N, R)) / u[None, :, None] * np.mean(u)),
            "W2": bf(np.random.standard_normal((R, I)) * 0.5 * np.sqrt(N) / (RM * np.sqrt(R))),
            "b2": bf(np.random.standard_normal(I) * 0.1)}


def reference(flows, x_gcn1, W2, b2):
    A = f64(flows)
    deg = A.sum(axis=1)
    dinv = np.where(deg > 0, 1.0 / np.sqrt(np.where(deg > 0, deg, 1.0)), 0.0)
    xw = f64(x_gcn1) @ f64(W2)
    msg = xw * dinv[..., None]
    out = mxq(A, 1, "e4m3").transpose(0, 2, 1) @ mxq(msg, 1, "e4m3")
    return out * dinv[..., None] + f64(b2)

@@ -1,0 +1,253 @@
+from contextlib import ExitStack
+
+import concourse.mybir as mybir
+from concourse.masks import make_identity
+
+F32 = mybir.dt.float32
+BF16 = mybir.dt.bfloat16
+U32 = mybir.dt.uint32
+U8 = mybir.dt.uint8
+FP8X4 = mybir.dt.float8_e4m3fn_x4
+ALU = mybir.AluOpType
+AXIS = mybir.AxisListType
+
+P = 128
+PACK = 4
+GRAPHS = 2
+NODES = 2048
+FEATURES = 128
+CHANNELS = 256
+PASSES = NODES // (P * PACK)
+NODE_TILES = NODES // P
+UNIT = 512
+UNITS = NODES // UNIT
+VECTOR_COLUMNS = UNIT // 4
+RUN = 4
+HALF = CHANNELS // 2
+STORE_TILES = 4
+
+FLOPS = 2 * GRAPHS * NODES * NODES * CHANNELS + 2 * GRAPHS * NODES * FEATURES * CHANNELS
+
+
+def tile_encoder_flows_pb_kernel(tc, flows, x_gcn1, W2, b2, out):
+    nc = tc.nc
+    with ExitStack() as ctx:
+        const = ctx.enter_context(tc.tile_pool(name="const", bufs=1))
+        keep = ctx.enter_context(tc.tile_pool(name="keep", bufs=1))
+        raw_pool = ctx.enter_context(tc.tile_pool(name="raw", bufs=5))
+        grouped_pool = ctx.enter_context(tc.tile_pool(name="grouped", bufs=4))
+        small = ctx.enter_context(tc.tile_pool(name="small", bufs=2))
+        result_pool = ctx.enter_context(tc.tile_pool(name="result", bufs=3))
+        deg_psum = ctx.enter_context(tc.psum_pool(name="deg_psum", bufs=2))
+        work_psum = ctx.enter_context(tc.psum_pool(name="work_psum", bufs=2))
+        acc_psum = ctx.enter_context(tc.psum_pool(name="acc_psum", bufs=4))
+
+        ones = const.tile([P, P], BF16)
+        nc.vector.memset(ones[:], 1.0)
+        identity = const.tile([P, P], BF16)
+        make_identity(nc, identity[:])
+        scratch = const.tile([P, 1], F32)
+        nc.vector.memset(scratch[:], 1.0)
+        nc.scalar.sqrt(scratch[:], scratch[:])
+
+        flow_codes = [
+            keep.tile([P, PASSES, NODES], U32, name="flow_codes%d" % g, align_bytes=64)
+            for g in range(GRAPHS)
+        ]
+        flow_scales = [
+            keep.tile([P, PASSES, NODES], U8, name="flow_scales%d" % g, align_bytes=64)
+            for g in range(GRAPHS)
+        ]
+        msg_codes = [
+            keep.tile([P, PASSES, CHANNELS], U32, name="msg_codes%d" % g, align_bytes=64)
+            for g in range(GRAPHS)
+        ]
+        msg_scales = [
+            keep.tile([P, PASSES, CHANNELS], U8, name="msg_scales%d" % g, align_bytes=64)
+            for g in range(GRAPHS)
+        ]
+        x_rows = [keep.tile([P, NODE_TILES, FEATURES], BF16, name="x_rows%d" % g) for g in range(GRAPHS)]
+        x_cols = [keep.tile([P, NODE_TILES, P], BF16, name="x_cols%d" % g) for g in range(GRAPHS)]
+        w2_sb = const.tile([FEATURES, CHANNELS], BF16)
+        bias_row = const.tile([P, CHANNELS], BF16)
+        bias = const.tile([P, CHANNELS], F32)
+
+        raw = {}
+        deg_parts = {}
+        dinv = {}
+
+        def load_rows(g, a):
+            raw[g, a] = raw_pool.tile([P, PACK, NODES], BF16, name="raw")
+            for t in range(PACK):
+                first = (a * PACK + t) * P
+                nc.sync.dma_start(out=raw[g, a][:, t, :], in_=flows[g, first : first + P, :])
+
+        def load_rows_by_units(g, a):
+            raw[g, a] = raw_pool.tile([P, PACK, NODES], BF16, name="raw")
+            rows = flows[g, a * P * PACK : (a + 1) * P * PACK, :].rearrange("(t p) c -> p t c", p=P)
+            for u in range(UNITS):
+                cols = slice(u * UNIT, (u + 1) * UNIT)
+                nc.sync.dma_start(out=raw[g, a][:, :, cols], in_=rows[:, :, cols])
+
+        def load_features(g):
+            nc.sync.dma_start(out=x_rows[g][:], in_=x_gcn1[g].rearrange("(n p) k -> p n k", p=P))
+
+        def transpose_features(g):
+            for q in range(NODE_TILES // PACK):
+                turned = work_psum.tile([P, PACK, P], BF16, tag="work")
+                for j in range(PACK):
+                    nc.tensor.transpose(turned[:, j, :], x_rows[g][:, q * PACK + j, :], identity[:])
+                nc.vector.tensor_copy(out=x_cols[g][:, q * PACK : (q + 1) * PACK, :], in_=turned[:])
+
+        def degree_parts(g, a):
+            if a == 0:
+                deg_parts[g] = deg_psum.tile([P, NODE_TILES, NODE_TILES], F32, name="deg_parts")
+            for t in range(PACK):
+                for n in range(NODE_TILES):
+                    nc.tensor.matmul(
+                        out=deg_parts[g][:, n, a * PACK + t : a * PACK + t + 1],
+                        lhsT=raw[g, a][:, t, n * P : (n + 1) * P],
+                        rhs=ones[:, 0:1],
+                        start=True,
+                        stop=True,
+                    )
+
+        def regroup(copy, g, a, u, grouped, first, last):
+            copy(
+                out=grouped[:, first:last, :].rearrange("p (c i) t -> p c t i", i=RUN),
+                in_=raw[g, a][:, :, u * UNIT + first : u * UNIT + last].rearrange(
+                    "p t (c i) -> p c t i", i=RUN
+                ),
+            )
+
+        def regroup_unit(g, a, u):
+            grouped = grouped_pool.tile([P, UNIT, PACK], BF16, name="grouped", align_bytes=64)
+            regroup(nc.vector.tensor_copy, g, a, u, grouped, 0, VECTOR_COLUMNS)
+            regroup(nc.scalar.copy, g, a, u, grouped, VECTOR_COLUMNS, UNIT)
+            return grouped
+
+        def quantise_unit(g, a, u, grouped):
+            cols = slice(u * UNIT, (u + 1) * UNIT)
+            nc.vector.quantize_mx(
+                out=flow_codes[g][:, a, cols].bitcast(FP8X4),
+                scales=flow_scales[g][:, a, cols],
+                in_=grouped[:].rearrange("p c t -> p (c t)"),
+            )
+
+        def normalisers(g):
+            deg = small.tile([P, NODE_TILES], F32, name="deg")
+            nc.vector.tensor_reduce(out=deg[:], in_=deg_parts[g][:], axis=AXIS.X, op=ALU.add)
+            safe = small.tile([P, NODE_TILES], F32, name="safe")
+            nc.vector.scalar_tensor_tensor(
+                out=safe[:], in0=deg[:], scalar=0.0, in1=deg[:], op0=ALU.is_le, op1=ALU.add
+            )
+            root = small.tile([P, NODE_TILES], F32, name="root")
+            nc.scalar.sqrt(root[:], safe[:])
+            inverse = small.tile([P, NODE_TILES], F32, name="inverse")
+            nc.vector.reciprocal(inverse[:], root[:])
+            dinv[g] = small.tile([P, NODE_TILES], F32, name="dinv")
+            nc.vector.scalar_tensor_tensor(
+                out=dinv[g][:], in0=deg[:], scalar=0.0, in1=inverse[:], op0=ALU.is_gt, op1=ALU.mult
+            )
+
+        def messages(g):
+            grouped_msg = keep.tile([P, PASSES, CHANNELS, PACK], BF16, name="grouped_msg", align_bytes=64)
+            for a in range(PASSES):
+                for h in range(CHANNELS // HALF):
+                    xw = work_psum.tile([P, PACK, HALF], F32, tag="work")
+                    for t in range(PACK):
+                        nc.tensor.matmul(
+                            out=xw[:, t, :],
+                            lhsT=x_cols[g][:, a * PACK + t, :],
+                            rhs=w2_sb[:, h * HALF : (h + 1) * HALF],
+                            start=True,
+                            stop=True,
+                        )
+                    nc.vector.tensor_tensor(
+                        out=grouped_msg[:, a, h * HALF : (h + 1) * HALF, :],
+                        in0=xw[:].rearrange("p t i -> p i t"),
+                        in1=dinv[g][:, a * PACK : (a + 1) * PACK].unsqueeze(1).to_broadcast([P, HALF, PACK]),
+                        op=ALU.mult,
+                    )
+            nc.vector.quantize_mx(
+                out=msg_codes[g][:].rearrange("p a i -> p (a i)").bitcast(FP8X4),
+                scales=msg_scales[g][:].rearrange("p a i -> p (a i)"),
+                in_=grouped_msg[:].rearrange("p a i t -> p (a i t)"),
+            )
+
+        results = {}
+
+        def product(g, n):
+            acc = acc_psum.tile([P, CHANNELS], F32, name="acc")
+            for a in range(PASSES):
+                nc.tensor.matmul_mx(
+                    out=acc[:],
+                    lhsT=flow_codes[g][:, a, n * P : (n + 1) * P].bitcast(FP8X4),
+                    lhsT_scale=flow_scales[g][:, a, n * P : (n + 1) * P],
+                    rhs=msg_codes[g][:, a, :].bitcast(FP8X4),
+                    rhs_scale=msg_scales[g][:, a, :],
+                    start=(a == 0),
+                    stop=(a == PASSES - 1),
+                )
+            j = n % STORE_TILES
+            if j == 0:
+                results[g] = result_pool.tile([P, STORE_TILES, CHANNELS], F32, name="result")
+            nc.vector.scalar_tensor_tensor(
+                out=results[g][:, j, :],
+                in0=acc[:],
+                scalar=dinv[g][:, n : n + 1],
+                in1=bias[:],
+                op0=ALU.mult,
+                op1=ALU.add,
+            )
+            if j == STORE_TILES - 1:
+                first = (n - j) * P
+                nc.sync.dma_start(
+                    out=out[g, first : first + STORE_TILES * P, :].rearrange("(j p) i -> p j i", p=P),
+                    in_=results[g][:],
+                )
+
+        load_rows_by_units(0, 0)
+        nc.sync.dma_start(out=w2_sb[:], in_=W2)
+        nc.vector.memset(bias_row[:], 0.0)
+        nc.sync.dma_start(out=bias_row[0:1, :], in_=b2.unsqueeze(0))
+        load_features(0)
+        load_features(1)
+        for a in range(1, PASSES):
+            load_rows(0, a)
+        load_rows(1, 0)
+
+        waiting = []
+
+        def next_unit(g, a, u):
+            grouped = regroup_unit(g, a, u)
+            if waiting:
+                quantise_unit(*waiting.pop())
+            waiting.append((g, a, u, grouped))
+
+        for a in range(PASSES):
+            degree_parts(0, a)
+            for u in range(UNITS):
+                next_unit(0, a, u)
+            if a + 1 < PASSES:
+                load_rows(1, a + 1)
+            if a == 0:
+                spread = work_psum.tile([P, CHANNELS], F32, tag="work")
+                nc.tensor.matmul(out=spread[:], lhsT=ones[:], rhs=bias_row[:], start=True, stop=True)
+                nc.vector.tensor_copy(out=bias[:], in_=spread[:])
+                transpose_features(0)
+            if a == 1:
+                transpose_features(1)
+        normalisers(0)
+        messages(0)
+
+        for a in range(PASSES):
+            degree_parts(1, a)
+            for u in range(UNITS):
+                next_unit(1, a, u)
+                product(0, a * UNITS + u)
+        quantise_unit(*waiting.pop())
+        normalisers(1)
+        messages(1)
+        for n in range(NODE_TILES):
+            product(1, n)

@@ -21,10 +21,11 @@ PASSES = NODES // (P * PACK)
 NODE_TILES = NODES // P
 UNIT = 512
 UNITS = NODES // UNIT
-VECTOR_COLUMNS = UNIT // 4
+VECTOR_COLUMNS = (256, 64)
 RUN = 4
 HALF = CHANNELS // 2
 STORE_TILES = 4
+AHEAD = 2
 
 FLOPS = 2 * GRAPHS * NODES * NODES * CHANNELS + 2 * GRAPHS * NODES * FEATURES * CHANNELS
 
@@ -35,7 +36,7 @@ def tile_encoder_flows_pb_kernel(tc, flows, x_gcn1, W2, b2, out):
         const = ctx.enter_context(tc.tile_pool(name="const", bufs=1))
         keep = ctx.enter_context(tc.tile_pool(name="keep", bufs=1))
         raw_pool = ctx.enter_context(tc.tile_pool(name="raw", bufs=5))
-        grouped_pool = ctx.enter_context(tc.tile_pool(name="grouped", bufs=4))
+        grouped_pool = ctx.enter_context(tc.tile_pool(name="grouped", bufs=6))
         small = ctx.enter_context(tc.tile_pool(name="small", bufs=2))
         result_pool = ctx.enter_context(tc.tile_pool(name="result", bufs=3))
         deg_psum = ctx.enter_context(tc.psum_pool(name="deg_psum", bufs=2))
@@ -97,7 +98,7 @@ def tile_encoder_flows_pb_kernel(tc, flows, x_gcn1, W2, b2, out):
                 turned = work_psum.tile([P, PACK, P], BF16, tag="work")
                 for j in range(PACK):
                     nc.tensor.transpose(turned[:, j, :], x_rows[g][:, q * PACK + j, :], identity[:])
-                nc.vector.tensor_copy(out=x_cols[g][:, q * PACK : (q + 1) * PACK, :], in_=turned[:])
+                nc.scalar.copy(out=x_cols[g][:, q * PACK : (q + 1) * PACK, :], in_=turned[:])
 
         def degree_parts(g, a):
             if a == 0:
@@ -122,8 +123,9 @@ def tile_encoder_flows_pb_kernel(tc, flows, x_gcn1, W2, b2, out):
 
         def regroup_unit(g, a, u):
             grouped = grouped_pool.tile([P, UNIT, PACK], BF16, name="grouped", align_bytes=64)
-            regroup(nc.vector.tensor_copy, g, a, u, grouped, 0, VECTOR_COLUMNS)
-            regroup(nc.scalar.copy, g, a, u, grouped, VECTOR_COLUMNS, UNIT)
+            if VECTOR_COLUMNS[g] > 0:
+                regroup(nc.vector.tensor_copy, g, a, u, grouped, 0, VECTOR_COLUMNS[g])
+            regroup(nc.scalar.copy, g, a, u, grouped, VECTOR_COLUMNS[g], UNIT)
             return grouped
 
         def quantise_unit(g, a, u, grouped):
@@ -175,13 +177,14 @@ def tile_encoder_flows_pb_kernel(tc, flows, x_gcn1, W2, b2, out):
                 in_=grouped_msg[:].rearrange("p a i t -> p (a i t)"),
             )
 
+        acc = {}
         results = {}
 
-        def product(g, n):
-            acc = acc_psum.tile([P, CHANNELS], F32, name="acc")
+        def multiply(g, n):
+            acc[g, n] = acc_psum.tile([P, CHANNELS], F32, name="acc")
             for a in range(PASSES):
                 nc.tensor.matmul_mx(
-                    out=acc[:],
+                    out=acc[g, n][:],
                     lhsT=flow_codes[g][:, a, n * P : (n + 1) * P].bitcast(FP8X4),
                     lhsT_scale=flow_scales[g][:, a, n * P : (n + 1) * P],
                     rhs=msg_codes[g][:, a, :].bitcast(FP8X4),
@@ -189,12 +192,14 @@ def tile_encoder_flows_pb_kernel(tc, flows, x_gcn1, W2, b2, out):
                     start=(a == 0),
                     stop=(a == PASSES - 1),
                 )
+
+        def finish(g, n):
             j = n % STORE_TILES
             if j == 0:
                 results[g] = result_pool.tile([P, STORE_TILES, CHANNELS], F32, name="result")
             nc.vector.scalar_tensor_tensor(
                 out=results[g][:, j, :],
-                in0=acc[:],
+                in0=acc[g, n][:],
                 scalar=dinv[g][:, n : n + 1],
                 in1=bias[:],
                 op0=ALU.mult,
@@ -212,9 +217,9 @@ def tile_encoder_flows_pb_kernel(tc, flows, x_gcn1, W2, b2, out):
         nc.vector.memset(bias_row[:], 0.0)
         nc.sync.dma_start(out=bias_row[0:1, :], in_=b2.unsqueeze(0))
         load_features(0)
-        load_features(1)
         for a in range(1, PASSES):
             load_rows(0, a)
+        load_features(1)
         load_rows(1, 0)
 
         waiting = []
@@ -226,7 +231,8 @@ def tile_encoder_flows_pb_kernel(tc, flows, x_gcn1, W2, b2, out):
             waiting.append((g, a, u, grouped))
 
         for a in range(PASSES):
-            degree_parts(0, a)
+            with tc.high_priority():
+                degree_parts(0, a)
             for u in range(UNITS):
                 next_unit(0, a, u)
             if a + 1 < PASSES:
@@ -236,18 +242,38 @@ def tile_encoder_flows_pb_kernel(tc, flows, x_gcn1, W2, b2, out):
                 nc.tensor.matmul(out=spread[:], lhsT=ones[:], rhs=bias_row[:], start=True, stop=True)
                 nc.vector.tensor_copy(out=bias[:], in_=spread[:])
                 transpose_features(0)
-            if a == 1:
-                transpose_features(1)
-        normalisers(0)
-        messages(0)
+        with tc.high_priority():
+            normalisers(0)
+            messages(0)
+        transpose_features(1)
 
-        for a in range(PASSES):
-            degree_parts(1, a)
+        for n in range(AHEAD):
+            multiply(0, n)
+        for a in range(PASSES // 2):
+            with tc.high_priority():
+                degree_parts(1, a)
             for u in range(UNITS):
                 next_unit(1, a, u)
-                product(0, a * UNITS + u)
-        quantise_unit(*waiting.pop())
-        normalisers(1)
-        messages(1)
-        for n in range(NODE_TILES):
-            product(1, n)
+                for n in range(2 * (a * UNITS + u), 2 * (a * UNITS + u) + 2):
+                    if n + AHEAD < NODE_TILES:
+                        multiply(0, n + AHEAD)
+                    finish(0, n)
+
+        with tc.high_priority():
+            for a in range(PASSES // 2, PASSES):
+                degree_parts(1, a)
+            normalisers(1)
+            messages(1)
+        tiles_of_unit = UNIT // P
+        for u in range(UNITS + 2):
+            if u < UNITS:
+                next_unit(1, PASSES - 2, u)
+                next_unit(1, PASSES - 1, u)
+            if u == UNITS:
+                quantise_unit(*waiting.pop())
+            if 2 <= u:
+                for n in range((u - 2) * tiles_of_unit, (u - 1) * tiles_of_unit):
+                    finish(1, n)
+            if 1 <= u <= UNITS:
+                for n in range((u - 1) * tiles_of_unit, u * tiles_of_unit):
+                    multiply(1, n)

@@ -24,7 +24,7 @@ UNITS = NODES // UNIT
 VECTOR_COLUMNS = (256, 64)
 RUN = 4
 HALF = CHANNELS // 2
-STORE_TILES = 4
+STORE_TILES = 2
 AHEAD = 2
 
 FLOPS = 2 * GRAPHS * NODES * NODES * CHANNELS + 2 * GRAPHS * NODES * FEATURES * CHANNELS
@@ -82,13 +82,6 @@ def tile_encoder_flows_pb_kernel(tc, flows, x_gcn1, W2, b2, out):
             for t in range(PACK):
                 first = (a * PACK + t) * P
                 nc.sync.dma_start(out=raw[g, a][:, t, :], in_=flows[g, first : first + P, :])
-
-        def load_rows_by_units(g, a):
-            raw[g, a] = raw_pool.tile([P, PACK, NODES], BF16, name="raw")
-            rows = flows[g, a * P * PACK : (a + 1) * P * PACK, :].rearrange("(t p) c -> p t c", p=P)
-            for u in range(UNITS):
-                cols = slice(u * UNIT, (u + 1) * UNIT)
-                nc.sync.dma_start(out=raw[g, a][:, :, cols], in_=rows[:, :, cols])
 
         def load_features(g):
             nc.sync.dma_start(out=x_rows[g][:], in_=x_gcn1[g].rearrange("(n p) k -> p n k", p=P))
@@ -171,11 +164,11 @@ def tile_encoder_flows_pb_kernel(tc, flows, x_gcn1, W2, b2, out):
                         in1=dinv[g][:, a * PACK : (a + 1) * PACK].unsqueeze(1).to_broadcast([P, HALF, PACK]),
                         op=ALU.mult,
                     )
-            nc.vector.quantize_mx(
-                out=msg_codes[g][:].rearrange("p a i -> p (a i)").bitcast(FP8X4),
-                scales=msg_scales[g][:].rearrange("p a i -> p (a i)"),
-                in_=grouped_msg[:].rearrange("p a i t -> p (a i t)"),
-            )
+                nc.vector.quantize_mx(
+                    out=msg_codes[g][:, a, :].bitcast(FP8X4),
+                    scales=msg_scales[g][:, a, :],
+                    in_=grouped_msg[:, a, :, :].rearrange("p i t -> p (i t)"),
+                )
 
         acc = {}
         results = {}
@@ -212,14 +205,13 @@ def tile_encoder_flows_pb_kernel(tc, flows, x_gcn1, W2, b2, out):
                     in_=results[g][:],
                 )
 
-        load_rows_by_units(0, 0)
+        load_rows(0, 0)
         nc.sync.dma_start(out=w2_sb[:], in_=W2)
         nc.vector.memset(bias_row[:], 0.0)
         nc.sync.dma_start(out=bias_row[0:1, :], in_=b2.unsqueeze(0))
         load_features(0)
         for a in range(1, PASSES):
             load_rows(0, a)
-        load_features(1)
         load_rows(1, 0)
 
         waiting = []
@@ -242,28 +234,31 @@ def tile_encoder_flows_pb_kernel(tc, flows, x_gcn1, W2, b2, out):
                 nc.tensor.matmul(out=spread[:], lhsT=ones[:], rhs=bias_row[:], start=True, stop=True)
                 nc.vector.tensor_copy(out=bias[:], in_=spread[:])
                 transpose_features(0)
+        load_features(1)
         with tc.high_priority():
             normalisers(0)
             messages(0)
-        transpose_features(1)
 
-        for n in range(AHEAD):
-            multiply(0, n)
         for a in range(PASSES // 2):
             with tc.high_priority():
                 degree_parts(1, a)
             for u in range(UNITS):
                 next_unit(1, a, u)
-                for n in range(2 * (a * UNITS + u), 2 * (a * UNITS + u) + 2):
-                    if n + AHEAD < NODE_TILES:
-                        multiply(0, n + AHEAD)
-                    finish(0, n)
 
         with tc.high_priority():
             for a in range(PASSES // 2, PASSES):
                 degree_parts(1, a)
+            transpose_features(1)
             normalisers(1)
             messages(1)
+
+        for n in range(AHEAD):
+            multiply(0, n)
+        for n in range(NODE_TILES):
+            if n + AHEAD < NODE_TILES:
+                multiply(0, n + AHEAD)
+            finish(0, n)
+
         tiles_of_unit = UNIT // P
         for u in range(UNITS + 2):
             if u < UNITS:

@@ -39,8 +39,8 @@ def tile_encoder_flows_pb_kernel(tc, flows, x_gcn1, W2, b2, out):
         grouped_pool = ctx.enter_context(tc.tile_pool(name="grouped", bufs=6))
         small = ctx.enter_context(tc.tile_pool(name="small", bufs=2))
         result_pool = ctx.enter_context(tc.tile_pool(name="result", bufs=3))
-        deg_psum = ctx.enter_context(tc.psum_pool(name="deg_psum", bufs=2))
-        work_psum = ctx.enter_context(tc.psum_pool(name="work_psum", bufs=2))
+        deg_psum = ctx.enter_context(tc.psum_pool(name="deg_psum", bufs=1))
+        work_psum = ctx.enter_context(tc.psum_pool(name="work_psum", bufs=3))
         acc_psum = ctx.enter_context(tc.psum_pool(name="acc_psum", bufs=4))
 
         ones = const.tile([P, P], BF16)

from contextlib import ExitStack

import concourse.mybir as mybir
from concourse.masks import make_identity

F32 = mybir.dt.float32
BF16 = mybir.dt.bfloat16
U32 = mybir.dt.uint32
U8 = mybir.dt.uint8
FP8X4 = mybir.dt.float8_e4m3fn_x4
ALU = mybir.AluOpType
AXIS = mybir.AxisListType

P = 128
PACK = 4
GRAPHS = 2
NODES = 2048
FEATURES = 128
CHANNELS = 256
PASSES = NODES // (P * PACK)
NODE_TILES = NODES // P
UNIT = 512
UNITS = NODES // UNIT
VECTOR_COLUMNS = (256, 64)
RUN = 4
HALF = CHANNELS // 2
STORE_TILES = 2
AHEAD = 2

FLOPS = 2 * GRAPHS * NODES * NODES * CHANNELS + 2 * GRAPHS * NODES * FEATURES * CHANNELS


def tile_encoder_flows_pb_kernel(tc, flows, x_gcn1, W2, b2, out):
    nc = tc.nc
    with ExitStack() as ctx:
        const = ctx.enter_context(tc.tile_pool(name="const", bufs=1))
        keep = ctx.enter_context(tc.tile_pool(name="keep", bufs=1))
        raw_pool = ctx.enter_context(tc.tile_pool(name="raw", bufs=5))
        grouped_pool = ctx.enter_context(tc.tile_pool(name="grouped", bufs=6))
        small = ctx.enter_context(tc.tile_pool(name="small", bufs=2))
        result_pool = ctx.enter_context(tc.tile_pool(name="result", bufs=3))
        deg_psum = ctx.enter_context(tc.psum_pool(name="deg_psum", bufs=1))
        work_psum = ctx.enter_context(tc.psum_pool(name="work_psum", bufs=3))
        acc_psum = ctx.enter_context(tc.psum_pool(name="acc_psum", bufs=4))

        ones = const.tile([P, P], BF16)
        nc.vector.memset(ones[:], 1.0)
        identity = const.tile([P, P], BF16)
        make_identity(nc, identity[:])
        scratch = const.tile([P, 1], F32)
        nc.vector.memset(scratch[:], 1.0)
        nc.scalar.sqrt(scratch[:], scratch[:])

        flow_codes = [
            keep.tile([P, PASSES, NODES], U32, name="flow_codes%d" % g, align_bytes=64)
            for g in range(GRAPHS)
        ]
        flow_scales = [
            keep.tile([P, PASSES, NODES], U8, name="flow_scales%d" % g, align_bytes=64)
            for g in range(GRAPHS)
        ]
        msg_codes = [
            keep.tile([P, PASSES, CHANNELS], U32, name="msg_codes%d" % g, align_bytes=64)
            for g in range(GRAPHS)
        ]
        msg_scales = [
            keep.tile([P, PASSES, CHANNELS], U8, name="msg_scales%d" % g, align_bytes=64)
            for g in range(GRAPHS)
        ]
        x_rows = [keep.tile([P, NODE_TILES, FEATURES], BF16, name="x_rows%d" % g) for g in range(GRAPHS)]
        x_cols = [keep.tile([P, NODE_TILES, P], BF16, name="x_cols%d" % g) for g in range(GRAPHS)]
        w2_sb = const.tile([FEATURES, CHANNELS], BF16)
        bias_row = const.tile([P, CHANNELS], BF16)
        bias = const.tile([P, CHANNELS], F32)

        raw = {}
        deg_parts = {}
        dinv = {}

        def load_rows(g, a):
            raw[g, a] = raw_pool.tile([P, PACK, NODES], BF16, name="raw")
            for t in range(PACK):
                first = (a * PACK + t) * P
                nc.sync.dma_start(out=raw[g, a][:, t, :], in_=flows[g, first : first + P, :])

        def load_features(g):
            nc.sync.dma_start(out=x_rows[g][:], in_=x_gcn1[g].rearrange("(n p) k -> p n k", p=P))

        def transpose_features(g):
            for q in range(NODE_TILES // PACK):
                turned = work_psum.tile([P, PACK, P], BF16, tag="work")
                for j in range(PACK):
                    nc.tensor.transpose(turned[:, j, :], x_rows[g][:, q * PACK + j, :], identity[:])
                nc.scalar.copy(out=x_cols[g][:, q * PACK : (q + 1) * PACK, :], in_=turned[:])

        def degree_parts(g, a):
            if a == 0:
                deg_parts[g] = deg_psum.tile([P, NODE_TILES, NODE_TILES], F32, name="deg_parts")
            for t in range(PACK):
                for n in range(NODE_TILES):
                    nc.tensor.matmul(
                        out=deg_parts[g][:, n, a * PACK + t : a * PACK + t + 1],
                        lhsT=raw[g, a][:, t, n * P : (n + 1) * P],
                        rhs=ones[:, 0:1],
                        start=True,
                        stop=True,
                    )

        def regroup(copy, g, a, u, grouped, first, last):
            copy(
                out=grouped[:, first:last, :].rearrange("p (c i) t -> p c t i", i=RUN),
                in_=raw[g, a][:, :, u * UNIT + first : u * UNIT + last].rearrange(
                    "p t (c i) -> p c t i", i=RUN
                ),
            )

        def regroup_unit(g, a, u):
            grouped = grouped_pool.tile([P, UNIT, PACK], BF16, name="grouped", align_bytes=64)
            if VECTOR_COLUMNS[g] > 0:
                regroup(nc.vector.tensor_copy, g, a, u, grouped, 0, VECTOR_COLUMNS[g])
            regroup(nc.scalar.copy, g, a, u, grouped, VECTOR_COLUMNS[g], UNIT)
            return grouped

        def quantise_unit(g, a, u, grouped):
            cols = slice(u * UNIT, (u + 1) * UNIT)
            nc.vector.quantize_mx(
                out=flow_codes[g][:, a, cols].bitcast(FP8X4),
                scales=flow_scales[g][:, a, cols],
                in_=grouped[:].rearrange("p c t -> p (c t)"),
            )

        def normalisers(g):
            deg = small.tile([P, NODE_TILES], F32, name="deg")
            nc.vector.tensor_reduce(out=deg[:], in_=deg_parts[g][:], axis=AXIS.X, op=ALU.add)
            safe = small.tile([P, NODE_TILES], F32, name="safe")
            nc.vector.scalar_tensor_tensor(
                out=safe[:], in0=deg[:], scalar=0.0, in1=deg[:], op0=ALU.is_le, op1=ALU.add
            )
            root = small.tile([P, NODE_TILES], F32, name="root")
            nc.scalar.sqrt(root[:], safe[:])
            inverse = small.tile([P, NODE_TILES], F32, name="inverse")
            nc.vector.reciprocal(inverse[:], root[:])
            dinv[g] = small.tile([P, NODE_TILES], F32, name="dinv")
            nc.vector.scalar_tensor_tensor(
                out=dinv[g][:], in0=deg[:], scalar=0.0, in1=inverse[:], op0=ALU.is_gt, op1=ALU.mult
            )

        def messages(g):
            grouped_msg = keep.tile([P, PASSES, CHANNELS, PACK], BF16, name="grouped_msg", align_bytes=64)
            for a in range(PASSES):
                for h in range(CHANNELS // HALF):
                    xw = work_psum.tile([P, PACK, HALF], F32, tag="work")
                    for t in range(PACK):
                        nc.tensor.matmul(
                            out=xw[:, t, :],
                            lhsT=x_cols[g][:, a * PACK + t, :],
                            rhs=w2_sb[:, h * HALF : (h + 1) * HALF],
                            start=True,
                            stop=True,
                        )
                    nc.vector.tensor_tensor(
                        out=grouped_msg[:, a, h * HALF : (h + 1) * HALF, :],
                        in0=xw[:].rearrange("p t i -> p i t"),
                        in1=dinv[g][:, a * PACK : (a + 1) * PACK].unsqueeze(1).to_broadcast([P, HALF, PACK]),
                        op=ALU.mult,
                    )
                nc.vector.quantize_mx(
                    out=msg_codes[g][:, a, :].bitcast(FP8X4),
                    scales=msg_scales[g][:, a, :],
                    in_=grouped_msg[:, a, :, :].rearrange("p i t -> p (i t)"),
                )

        acc = {}
        results = {}

        def multiply(g, n):
            acc[g, n] = acc_psum.tile([P, CHANNELS], F32, name="acc")
            for a in range(PASSES):
                nc.tensor.matmul_mx(
                    out=acc[g, n][:],
                    lhsT=flow_codes[g][:, a, n * P : (n + 1) * P].bitcast(FP8X4),
                    lhsT_scale=flow_scales[g][:, a, n * P : (n + 1) * P],
                    rhs=msg_codes[g][:, a, :].bitcast(FP8X4),
                    rhs_scale=msg_scales[g][:, a, :],
                    start=(a == 0),
                    stop=(a == PASSES - 1),
                )

        def finish(g, n):
            j = n % STORE_TILES
            if j == 0:
                results[g] = result_pool.tile([P, STORE_TILES, CHANNELS], F32, name="result")
            nc.vector.scalar_tensor_tensor(
                out=results[g][:, j, :],
                in0=acc[g, n][:],
                scalar=dinv[g][:, n : n + 1],
                in1=bias[:],
                op0=ALU.mult,
                op1=ALU.add,
            )
            if j == STORE_TILES - 1:
                first = (n - j) * P
                nc.sync.dma_start(
                    out=out[g, first : first + STORE_TILES * P, :].rearrange("(j p) i -> p j i", p=P),
                    in_=results[g][:],
                )

        load_rows(0, 0)
        nc.sync.dma_start(out=w2_sb[:], in_=W2)
        nc.vector.memset(bias_row[:], 0.0)
        nc.sync.dma_start(out=bias_row[0:1, :], in_=b2.unsqueeze(0))
        load_features(0)
        for a in range(1, PASSES):
            load_rows(0, a)
        load_rows(1, 0)

        waiting = []

        def next_unit(g, a, u):
            grouped = regroup_unit(g, a, u)
            if waiting:
                quantise_unit(*waiting.pop())
            waiting.append((g, a, u, grouped))

        for a in range(PASSES):
            with tc.high_priority():
                degree_parts(0, a)
            for u in range(UNITS):
                next_unit(0, a, u)
            if a + 1 < PASSES:
                load_rows(1, a + 1)
            if a == 0:
                spread = work_psum.tile([P, CHANNELS], F32, tag="work")
                nc.tensor.matmul(out=spread[:], lhsT=ones[:], rhs=bias_row[:], start=True, stop=True)
                nc.vector.tensor_copy(out=bias[:], in_=spread[:])
                transpose_features(0)
        load_features(1)
        with tc.high_priority():
            normalisers(0)
            messages(0)

        for a in range(PASSES // 2):
            with tc.high_priority():
                degree_parts(1, a)
            for u in range(UNITS):
                next_unit(1, a, u)

        with tc.high_priority():
            for a in range(PASSES // 2, PASSES):
                degree_parts(1, a)
            transpose_features(1)
            normalisers(1)
            messages(1)

        for n in range(AHEAD):
            multiply(0, n)
        for n in range(NODE_TILES):
            if n + AHEAD < NODE_TILES:
                multiply(0, n + AHEAD)
            finish(0, n)

        tiles_of_unit = UNIT // P
        for u in range(UNITS + 2):
            if u < UNITS:
                next_unit(1, PASSES - 2, u)
                next_unit(1, PASSES - 1, u)
            if u == UNITS:
                quantise_unit(*waiting.pop())
            if 2 <= u:
                for n in range((u - 2) * tiles_of_unit, (u - 1) * tiles_of_unit):
                    finish(1, n)
            if 1 <= u <= UNITS:
                for n in range((u - 1) * tiles_of_unit, u * tiles_of_unit):
                    multiply(1, n)
